import numpy as np
import ml_dtypes


def mxq(x, axis, fmt="e4m3"):
    dtype, down = {"e4m3": (ml_dtypes.float8_e4m3fn, 7), "e5m2": (ml_dtypes.float8_e5m2, 14)}[fmt]
    v = np.moveaxis(np.asarray(x, np.float32).astype(ml_dtypes.bfloat16).astype(np.float64), axis, -1)
    blocks = v.reshape(v.shape[:-1] + (-1, 32))
    amax = np.abs(blocks).max(-1, keepdims=True)
    byte = np.maximum(np.where(amax > 0, np.frexp(amax)[1] - 1 + 127, 0) - down, 1)
    scale = np.exp2(byte - 127.0)
    codes = (blocks / scale).astype(np.float32).astype(dtype).astype(np.float64)
    return np.moveaxis((codes * scale).reshape(v.shape), -1, axis)


WIDE = False


def mx_kscale(k):
    if not WIDE:
        return np.ones(k)
    levels = np.array([10, -10, 5, -5, 0])
    if k % 512:
        return np.exp2(np.random.permutation(np.resize(levels, k // 32))).repeat(32)
    a = np.empty((k // 512, 16))
    for p in range(k // 512):
        a[p, :8] = np.random.permutation(np.resize(levels, 8))
        for g in range(8):
            far = levels[np.abs(levels - a[p, g]) >= 10]
            a[p, g + 8] = far[np.random.randint(len(far))]
    return np.exp2(a.ravel()).repeat(32)


BF16 = ml_dtypes.bfloat16


def bf(x):
    return np.asarray(x, np.float32).astype(BF16)


def f64(x):
    return np.asarray(x).astype(np.float64)


T, B, NJ, D, E, HD, R = 128, 4, 16, 1024, 512, 128, 128
BJ = B * NJ
SCALING = 2.0


def setup_inputs():
    s = mx_kscale(D)
    return {"query": bf(np.random.standard_normal((T, BJ, D)) * s),
            "m": bf(np.random.standard_normal((B, T, D)) * s),
            "w_q": bf(np.random.standard_normal((E, D)) * 0.8 / np.sqrt(D) / s),
            "b_q": bf(np.random.standard_normal(E) * 0.2),
            "A_q": bf(np.random.standard_normal((R, D)) / np.sqrt(D) / s),
            "B_q": bf(np.random.standard_normal((E, R)) * 0.3 / np.sqrt(R))}


def reference(query, m, w_q, b_q, A_q, B_q):
    m_exp = np.broadcast_to(f64(m).transpose(1, 0, 2)[:, :, None, :], (T, B, NJ, D)).reshape(T, BJ, D)
    q_in = f64(query) + m_exp
    wq_eff = f64(w_q) + (f64(B_q) @ f64(A_q)) * SCALING
    return (mxq(q_in, 2, "e4m3") @ mxq(wq_eff, 1, "e4m3").T) + f64(b_q)

@@ -1,0 +1,260 @@
+from contextlib import ExitStack
+
+import concourse.mybir as mybir
+from concourse.masks import make_identity
+
+BF16 = mybir.dt.bfloat16
+F32 = mybir.dt.float32
+U32 = mybir.dt.uint32
+U8 = mybir.dt.uint8
+FP8X4 = mybir.dt.float8_e4m3fn_x4
+ADD = mybir.AluOpType.add
+
+P = 128
+FRAMES = 128
+BATCH = 4
+JOINTS = 16
+ROWS = BATCH * JOINTS
+FEATURES = 1024
+OUTPUTS = 512
+RANK = 128
+LORA_SCALE = 2.0
+
+PACK = 4
+PASSES = FEATURES // (P * PACK)
+WORDS = FEATURES // 2
+PAIR = 2
+HALVES = 2
+OUTPUT_BLOCKS = OUTPUTS // P
+
+CHUNK = 4
+N_CHUNKS = ROWS // CHUNK
+CHUNKS_PER_BATCH = JOINTS // CHUNK
+LEAD = 3
+DETOUR = 1
+
+FLOPS = 2 * FRAMES * ROWS * FEATURES * OUTPUTS + 2 * OUTPUTS * RANK * FEATURES
+
+
+def turn_rows(nc, bank, row_words, identity):
+    for u in range(HALVES):
+        for g in range(PASSES):
+            nc.tensor.transpose(
+                bank[:, (u * PASSES + g) * P : (u * PASSES + g + 1) * P],
+                row_words[:, g * HALVES * P + u : (g + 1) * HALVES * P : HALVES],
+                identity,
+            )
+
+
+def tile_inversiontemporalmha_pa_t_kernel(tc, query, m, w_q, b_q, A_q, B_q, out):
+    nc = tc.nc
+    with ExitStack() as stack:
+        keep = stack.enter_context(tc.tile_pool(name="keep", bufs=1))
+        q_pool = stack.enter_context(tc.tile_pool(name="q", bufs=N_CHUNKS))
+        grouped_pool = stack.enter_context(tc.tile_pool(name="grouped", bufs=2))
+        packed_pool = stack.enter_context(tc.tile_pool(name="packed", bufs=LEAD + 1))
+        turn_psum = stack.enter_context(tc.psum_pool(name="turn_psum", bufs=CHUNK))
+        sum_psum = stack.enter_context(tc.psum_pool(name="sum_psum", bufs=CHUNK))
+
+        identity_f32 = keep.tile([P, P], F32)
+        m_turned = keep.tile([P, BATCH, WORDS], F32)
+        w_codes = keep.tile([P, PASSES * OUTPUTS], U32, align_bytes=64)
+        w_scales = keep.tile([P, PASSES * OUTPUTS], U8, align_bytes=64)
+        bias = keep.tile([P, OUTPUTS], F32)
+        q_chunks = []
+        for c in range(N_CHUNKS):
+            q_rows = q_pool.tile([P, CHUNK, FEATURES], BF16)
+            q_chunks.append(q_rows)
+
+        def turn(c):
+            banks = []
+            for i in range(CHUNK):
+                bank = turn_psum.tile([P, WORDS], F32, tag="turn")
+                turn_rows(nc, bank, q_chunks[c][:, i, :].bitcast(F32), identity_f32[:])
+                banks.append(bank)
+            return banks
+
+        def add_motion(c, banks):
+            b = c // CHUNKS_PER_BATCH
+            grouped = grouped_pool.tile([P, CHUNK, FEATURES], BF16, align_bytes=64)
+            for i in range(CHUNK):
+                nc.vector.tensor_tensor(
+                    out=grouped[:, i, :].rearrange("p (x u e) -> p x u e", u=HALVES, e=PAIR),
+                    in0=banks[i][:].bitcast(BF16).rearrange("p (u x e) -> p x u e", u=HALVES, e=PAIR),
+                    in1=m_turned[:, b, :].bitcast(BF16).rearrange("p (x u e) -> p x u e", u=HALVES, e=PAIR),
+                    op=ADD,
+                )
+            return grouped
+
+        def quantise(grouped):
+            codes = packed_pool.tile([P, CHUNK * PASSES * FRAMES], U32, align_bytes=64)
+            scales = packed_pool.tile([P, CHUNK * PASSES * FRAMES], U8, align_bytes=64)
+            nc.vector.quantize_mx(
+                out=codes[:].bitcast(FP8X4),
+                scales=scales[:],
+                in_=grouped[:].rearrange("p i n -> p (i n)"),
+            )
+            return codes, scales
+
+        packed = []
+
+        with tc.tile_pool(name="build", bufs=1) as build:
+            def load_motion(b):
+                nc.sync.dma_start(out=m_rows[:, b, :], in_=m[b, :, :])
+
+            def load_query(c, step):
+                for i in range(0, CHUNK, step):
+                    nc.sync.dma_start(
+                        out=q_chunks[c][:, i : i + step, :],
+                        in_=query[:, c * CHUNK + i : c * CHUNK + i + step, :],
+                    )
+
+            m_rows = build.tile([P, BATCH, FEATURES], BF16)
+            load_motion(0)
+            load_query(0, 1)
+            for c in range(1, LEAD - 1):
+                load_query(c, CHUNK)
+            b_rows = build.tile([P, OUTPUT_BLOCKS, RANK], BF16)
+            nc.sync.dma_start(out=b_rows[:], in_=B_q.rearrange("(h o) r -> o h r", o=P))
+            a_rows = build.tile([P, FEATURES], BF16)
+            nc.sync.dma_start(out=a_rows[:], in_=A_q)
+            w_rows = build.tile([P, OUTPUT_BLOCKS, FEATURES], BF16)
+            nc.sync.dma_start(out=w_rows[:], in_=w_q.rearrange("(h o) k -> o h k", o=P))
+            bias_row = build.tile([P, OUTPUTS], BF16)
+            nc.vector.memset(bias_row[:], 0.0)
+            nc.sync.dma_start(out=bias_row[0:1, :], in_=b_q.rearrange("(one o) -> one o", one=1))
+            for c in range(LEAD - 1, CHUNKS_PER_BATCH):
+                load_query(c, CHUNK)
+            for b in range(1, BATCH):
+                load_motion(b)
+            for c in range(CHUNKS_PER_BATCH, N_CHUNKS):
+                load_query(c, CHUNK)
+
+            make_identity(nc, identity_f32[:])
+            identity_bf16 = build.tile([P, P], BF16)
+            make_identity(nc, identity_bf16[:])
+            ones = build.tile([P, P], BF16)
+            nc.vector.memset(ones[:], 1.0)
+
+            def turn_motion(b):
+                bank = turn_psum.tile([P, WORDS], F32, tag="turn")
+                turn_rows(nc, bank, m_rows[:, b, :].bitcast(F32), identity_f32[:])
+                nc.scalar.copy(
+                    out=m_turned[:, b, :].rearrange("p (x u) -> p x u", u=HALVES),
+                    in_=bank[:].rearrange("p (u x) -> p x u", u=HALVES),
+                )
+
+            def prepare(c):
+                packed.append(quantise(add_motion(c, turn(c))))
+
+            w_grouped = build.tile([P, PASSES, OUTPUTS, PACK], BF16, align_bytes=64)
+            b_turned = build.tile([P, OUTPUTS], BF16)
+            feature_order = "r (g p u e) -> r g u e p"
+
+            def build_w(g):
+                a_by_word = a_rows[:].rearrange(feature_order, g=PASSES, u=HALVES, e=PAIR)
+                for h in range(OUTPUT_BLOCKS):
+                    w_by_word = w_rows[:, h, :].rearrange(feature_order, g=PASSES, u=HALVES, e=PAIR)
+                    w_turned = sum_psum.tile([P, PACK * P], F32, tag="sum")
+                    for u in range(HALVES):
+                        for e in range(PAIR):
+                            j = PAIR * u + e
+                            plane = w_turned[:, j * P : (j + 1) * P]
+                            nc.tensor.matmul(
+                                out=plane,
+                                lhsT=a_by_word[:, g, u, e, :],
+                                rhs=b_turned[:, h * P : (h + 1) * P],
+                                start=True,
+                                stop=False,
+                            )
+                            nc.tensor.matmul(
+                                out=plane,
+                                lhsT=w_by_word[:, g, u, e, :],
+                                rhs=identity_bf16[:],
+                                start=False,
+                                stop=True,
+                            )
+                    nc.scalar.copy(
+                        out=w_grouped[:, g, h * P : (h + 1) * P, :],
+                        in_=w_turned[:].rearrange("p (j o) -> p o j", j=PACK),
+                    )
+                outputs = slice(g * OUTPUTS, (g + 1) * OUTPUTS)
+                nc.vector.quantize_mx(
+                    out=w_codes[:, outputs].bitcast(FP8X4),
+                    scales=w_scales[:, outputs],
+                    in_=w_grouped[:, g, :, :].rearrange("p o j -> p (o j)"),
+                )
+
+            turn_motion(0)
+            for c in range(LEAD - 1):
+                prepare(c)
+            b_turned_psum = turn_psum.tile([P, OUTPUTS], BF16, tag="turn")
+            for h in range(OUTPUT_BLOCKS):
+                nc.tensor.transpose(
+                    b_turned_psum[:, h * P : (h + 1) * P], b_rows[:, h, :], identity_bf16[:]
+                )
+            nc.scalar.mul(out=b_turned[:], in_=b_turned_psum[:], mul=LORA_SCALE)
+            build_w(0)
+            prepare(LEAD - 1)
+            build_w(1)
+
+            bias_psum = sum_psum.tile([P, OUTPUTS], F32, tag="sum")
+            nc.tensor.matmul(
+                out=bias_psum[:], lhsT=ones[:], rhs=bias_row[:], start=True, stop=True
+            )
+            nc.scalar.copy(out=bias[:], in_=bias_psum[:])
+
+            for b in range(1, BATCH):
+                turn_motion(b)
+
+        result_pool = stack.enter_context(tc.tile_pool(name="result", bufs=3))
+
+        def multiply(c):
+            codes, scales = packed[c]
+            sums = []
+            for i in range(CHUNK):
+                acc = sum_psum.tile([P, OUTPUTS], F32, tag="sum")
+                for g in range(PASSES):
+                    frames = slice((i * PASSES + g) * FRAMES, (i * PASSES + g + 1) * FRAMES)
+                    outputs = slice(g * OUTPUTS, (g + 1) * OUTPUTS)
+                    nc.tensor.matmul_mx(
+                        out=acc[:],
+                        lhsT=codes[:, frames].bitcast(FP8X4),
+                        lhsT_scale=scales[:, frames],
+                        rhs=w_codes[:, outputs].bitcast(FP8X4),
+                        rhs_scale=w_scales[:, outputs],
+                        start=(g == 0),
+                        stop=(g == PASSES - 1),
+                    )
+                sums.append(acc)
+            return sums
+
+        def finish(c, sums):
+            result = result_pool.tile([P, CHUNK, OUTPUTS], F32)
+            step = 1 if c == N_CHUNKS - 1 else CHUNK
+            for i in range(CHUNK):
+                if i < DETOUR:
+                    nc.scalar.copy(out=result[:, i, :], in_=sums[i][:])
+                    nc.gpsimd.tensor_tensor(
+                        out=result[:, i, :], in0=result[:, i, :], in1=bias[:], op=ADD
+                    )
+                else:
+                    nc.vector.tensor_tensor(
+                        out=result[:, i, :], in0=sums[i][:], in1=bias[:], op=ADD
+                    )
+                if (i + 1) % step == 0:
+                    nc.sync.dma_start(
+                        out=out[:, c * CHUNK + i + 1 - step : c * CHUNK + i + 1, :],
+                        in_=result[:, i + 1 - step : i + 1, :],
+                    )
+
+        for c in range(N_CHUNKS):
+            ahead = c + LEAD
+            if ahead < N_CHUNKS:
+                banks = turn(ahead)
+            sums = multiply(c)
+            if ahead < N_CHUNKS:
+                grouped = add_motion(ahead, banks)
+            finish(c, sums)
+            if ahead < N_CHUNKS:
+                packed.append(quantise(grouped))

@@ -25,236 +25,270 @@ PASSES = FEATURES // (P * PACK)
 WORDS = FEATURES // 2
 PAIR = 2
 HALVES = 2
+HALF = WORDS // HALVES
 OUTPUT_BLOCKS = OUTPUTS // P
 
 CHUNK = 4
 N_CHUNKS = ROWS // CHUNK
 CHUNKS_PER_BATCH = JOINTS // CHUNK
 LEAD = 3
-DETOUR = 1
+FIRST_SORTED = LEAD
+LOAD_AHEAD = 9
 
 FLOPS = 2 * FRAMES * ROWS * FEATURES * OUTPUTS + 2 * OUTPUTS * RANK * FEATURES
 
 
-def turn_rows(nc, bank, row_words, identity):
-    for u in range(HALVES):
-        for g in range(PASSES):
-            nc.tensor.transpose(
-                bank[:, (u * PASSES + g) * P : (u * PASSES + g + 1) * P],
-                row_words[:, g * HALVES * P + u : (g + 1) * HALVES * P : HALVES],
-                identity,
-            )
+def detour(c):
+    return (2, 3) if c < N_CHUNKS - LEAD else ()
 
 
 def tile_inversiontemporalmha_pa_t_kernel(tc, query, m, w_q, b_q, A_q, B_q, out):
     nc = tc.nc
     with ExitStack() as stack:
         keep = stack.enter_context(tc.tile_pool(name="keep", bufs=1))
-        q_pool = stack.enter_context(tc.tile_pool(name="q", bufs=N_CHUNKS))
+        q_pool = stack.enter_context(tc.tile_pool(name="q", bufs=LOAD_AHEAD))
+        sorted_pool = stack.enter_context(tc.tile_pool(name="sorted", bufs=2))
         grouped_pool = stack.enter_context(tc.tile_pool(name="grouped", bufs=2))
         packed_pool = stack.enter_context(tc.tile_pool(name="packed", bufs=LEAD + 1))
+        result_pool = stack.enter_context(tc.tile_pool(name="result", bufs=4))
         turn_psum = stack.enter_context(tc.psum_pool(name="turn_psum", bufs=CHUNK))
         sum_psum = stack.enter_context(tc.psum_pool(name="sum_psum", bufs=CHUNK))
+        build = stack.enter_context(tc.tile_pool(name="build", bufs=1))
+        stack.enter_context(tc.manual_schedule())
 
         identity_f32 = keep.tile([P, P], F32)
+        identity_bf16 = keep.tile([P, P], BF16)
+        ones = keep.tile([P, P], BF16)
         m_turned = keep.tile([P, BATCH, WORDS], F32)
         w_codes = keep.tile([P, PASSES * OUTPUTS], U32, align_bytes=64)
         w_scales = keep.tile([P, PASSES * OUTPUTS], U8, align_bytes=64)
         bias = keep.tile([P, OUTPUTS], F32)
-        q_chunks = []
-        for c in range(N_CHUNKS):
+        m_rows = build.tile([P, BATCH, FEATURES], BF16)
+        b_rows = build.tile([P, OUTPUT_BLOCKS, RANK], BF16)
+        a_rows = build.tile([P, FEATURES], BF16)
+        w_rows = build.tile([P, OUTPUT_BLOCKS, FEATURES], BF16)
+        bias_row = build.tile([P, OUTPUTS], BF16)
+        b_turned = build.tile([P, OUTPUTS], BF16)
+        w_grouped = build.tile([P, PASSES, OUTPUTS, PACK], BF16, align_bytes=64)
+
+        q_chunks, sorted_words, banks, grouped, packed, sums = {}, {}, {}, {}, {}, {}
+
+        def load_motion(b):
+            nc.sync.dma_start(out=m_rows[:, b, :], in_=m[b, :, :])
+
+        def load_query(c, step):
             q_rows = q_pool.tile([P, CHUNK, FEATURES], BF16)
-            q_chunks.append(q_rows)
-
-        def turn(c):
-            banks = []
-            for i in range(CHUNK):
-                bank = turn_psum.tile([P, WORDS], F32, tag="turn")
-                turn_rows(nc, bank, q_chunks[c][:, i, :].bitcast(F32), identity_f32[:])
-                banks.append(bank)
-            return banks
-
-        def add_motion(c, banks):
-            b = c // CHUNKS_PER_BATCH
-            grouped = grouped_pool.tile([P, CHUNK, FEATURES], BF16, align_bytes=64)
-            for i in range(CHUNK):
-                nc.vector.tensor_tensor(
-                    out=grouped[:, i, :].rearrange("p (x u e) -> p x u e", u=HALVES, e=PAIR),
-                    in0=banks[i][:].bitcast(BF16).rearrange("p (u x e) -> p x u e", u=HALVES, e=PAIR),
-                    in1=m_turned[:, b, :].bitcast(BF16).rearrange("p (x u e) -> p x u e", u=HALVES, e=PAIR),
-                    op=ADD,
+            q_chunks[c] = q_rows
+            for i in range(0, CHUNK, step):
+                nc.sync.dma_start(
+                    out=q_rows[:, i : i + step, :],
+                    in_=query[:, c * CHUNK + i : c * CHUNK + i + step, :],
                 )
-            return grouped
 
-        def quantise(grouped):
+        def sort_query(c):
+            words = sorted_pool.tile([P, HALVES, CHUNK * HALF], F32, tag="sorted")
+            sorted_words[c] = words
+            rows = q_chunks[c][:].rearrange("p i k -> p (i k)").bitcast(F32)
+            step = CHUNK // 2
+            for i in range(0, CHUNK, step):
+                nc.scalar.copy(
+                    out=words[:, :, i * HALF : (i + step) * HALF],
+                    in_=rows[:, i * WORDS : (i + step) * WORDS].rearrange(
+                        "p (n u) -> p u n", u=HALVES
+                    ),
+                )
+
+        def turn_rows(bank, words_of):
+            for u in range(HALVES):
+                for g in range(PASSES):
+                    nc.tensor.transpose(
+                        bank[:, (u * PASSES + g) * P : (u * PASSES + g + 1) * P],
+                        words_of(u, g),
+                        identity_f32[:],
+                    )
+
+        def every_second(row):
+            words = row.bitcast(F32)
+            return lambda u, g: words[:, g * HALVES * P + u : (g + 1) * HALVES * P : HALVES]
+
+        def turn(c, i):
+            bank = turn_psum.tile([P, WORDS], F32, tag="turn")
+            banks[c, i] = bank
+            if c < FIRST_SORTED:
+                turn_rows(bank, every_second(q_chunks[c][:, i, :]))
+            else:
+                words = sorted_words[c]
+                turn_rows(
+                    bank, lambda u, g: words[:, u, i * HALF + g * P : i * HALF + (g + 1) * P]
+                )
+
+        def turn_motion(b):
+            bank = sum_psum.tile([P, WORDS], F32, tag="sum")
+            turn_rows(bank, every_second(m_rows[:, b, :]))
+            nc.scalar.copy(
+                out=m_turned[:, b, :].rearrange("p (x u) -> p x u", u=HALVES),
+                in_=bank[:].rearrange("p (u x) -> p x u", u=HALVES),
+            )
+
+        def add_motion(c, i):
+            if i == 0:
+                pairs = grouped_pool.tile([P, CHUNK, FEATURES], BF16, align_bytes=64)
+                grouped[c] = pairs
+            b = c // CHUNKS_PER_BATCH
+            nc.vector.tensor_tensor(
+                out=grouped[c][:, i, :].rearrange("p (x u e) -> p x u e", u=HALVES, e=PAIR),
+                in0=banks[c, i][:].bitcast(BF16).rearrange("p (u x e) -> p x u e", u=HALVES, e=PAIR),
+                in1=m_turned[:, b, :].bitcast(BF16).rearrange("p (x u e) -> p x u e", u=HALVES, e=PAIR),
+                op=ADD,
+            )
+
+        def quantise(c):
             codes = packed_pool.tile([P, CHUNK * PASSES * FRAMES], U32, align_bytes=64)
             scales = packed_pool.tile([P, CHUNK * PASSES * FRAMES], U8, align_bytes=64)
+            packed[c] = (codes, scales)
             nc.vector.quantize_mx(
                 out=codes[:].bitcast(FP8X4),
                 scales=scales[:],
-                in_=grouped[:].rearrange("p i n -> p (i n)"),
+                in_=grouped[c][:].rearrange("p i n -> p (i n)"),
             )
-            return codes, scales
 
-        packed = []
-
-        with tc.tile_pool(name="build", bufs=1) as build:
-            def load_motion(b):
-                nc.sync.dma_start(out=m_rows[:, b, :], in_=m[b, :, :])
-
-            def load_query(c, step):
-                for i in range(0, CHUNK, step):
-                    nc.sync.dma_start(
-                        out=q_chunks[c][:, i : i + step, :],
-                        in_=query[:, c * CHUNK + i : c * CHUNK + i + step, :],
-                    )
-
-            m_rows = build.tile([P, BATCH, FEATURES], BF16)
-            load_motion(0)
-            load_query(0, 1)
-            for c in range(1, LEAD - 1):
-                load_query(c, CHUNK)
-            b_rows = build.tile([P, OUTPUT_BLOCKS, RANK], BF16)
-            nc.sync.dma_start(out=b_rows[:], in_=B_q.rearrange("(h o) r -> o h r", o=P))
-            a_rows = build.tile([P, FEATURES], BF16)
-            nc.sync.dma_start(out=a_rows[:], in_=A_q)
-            w_rows = build.tile([P, OUTPUT_BLOCKS, FEATURES], BF16)
-            nc.sync.dma_start(out=w_rows[:], in_=w_q.rearrange("(h o) k -> o h k", o=P))
-            bias_row = build.tile([P, OUTPUTS], BF16)
-            nc.vector.memset(bias_row[:], 0.0)
-            nc.sync.dma_start(out=bias_row[0:1, :], in_=b_q.rearrange("(one o) -> one o", one=1))
-            for c in range(LEAD - 1, CHUNKS_PER_BATCH):
-                load_query(c, CHUNK)
-            for b in range(1, BATCH):
-                load_motion(b)
-            for c in range(CHUNKS_PER_BATCH, N_CHUNKS):
-                load_query(c, CHUNK)
-
-            make_identity(nc, identity_f32[:])
-            identity_bf16 = build.tile([P, P], BF16)
-            make_identity(nc, identity_bf16[:])
-            ones = build.tile([P, P], BF16)
-            nc.vector.memset(ones[:], 1.0)
-
-            def turn_motion(b):
-                bank = turn_psum.tile([P, WORDS], F32, tag="turn")
-                turn_rows(nc, bank, m_rows[:, b, :].bitcast(F32), identity_f32[:])
-                nc.scalar.copy(
-                    out=m_turned[:, b, :].rearrange("p (x u) -> p x u", u=HALVES),
-                    in_=bank[:].rearrange("p (u x) -> p x u", u=HALVES),
-                )
-
-            def prepare(c):
-                packed.append(quantise(add_motion(c, turn(c))))
-
-            w_grouped = build.tile([P, PASSES, OUTPUTS, PACK], BF16, align_bytes=64)
-            b_turned = build.tile([P, OUTPUTS], BF16)
-            feature_order = "r (g p u e) -> r g u e p"
-
-            def build_w(g):
-                a_by_word = a_rows[:].rearrange(feature_order, g=PASSES, u=HALVES, e=PAIR)
-                for h in range(OUTPUT_BLOCKS):
-                    w_by_word = w_rows[:, h, :].rearrange(feature_order, g=PASSES, u=HALVES, e=PAIR)
-                    w_turned = sum_psum.tile([P, PACK * P], F32, tag="sum")
-                    for u in range(HALVES):
-                        for e in range(PAIR):
-                            j = PAIR * u + e
-                            plane = w_turned[:, j * P : (j + 1) * P]
-                            nc.tensor.matmul(
-                                out=plane,
-                                lhsT=a_by_word[:, g, u, e, :],
-                                rhs=b_turned[:, h * P : (h + 1) * P],
-                                start=True,
-                                stop=False,
-                            )
-                            nc.tensor.matmul(
-                                out=plane,
-                                lhsT=w_by_word[:, g, u, e, :],
-                                rhs=identity_bf16[:],
-                                start=False,
-                                stop=True,
-                            )
-                    nc.scalar.copy(
-                        out=w_grouped[:, g, h * P : (h + 1) * P, :],
-                        in_=w_turned[:].rearrange("p (j o) -> p o j", j=PACK),
-                    )
-                outputs = slice(g * OUTPUTS, (g + 1) * OUTPUTS)
-                nc.vector.quantize_mx(
-                    out=w_codes[:, outputs].bitcast(FP8X4),
-                    scales=w_scales[:, outputs],
-                    in_=w_grouped[:, g, :, :].rearrange("p o j -> p (o j)"),
-                )
-
-            turn_motion(0)
-            for c in range(LEAD - 1):
-                prepare(c)
-            b_turned_psum = turn_psum.tile([P, OUTPUTS], BF16, tag="turn")
+        def turn_lora():
+            bank = sum_psum.tile([P, OUTPUTS], BF16, tag="sum")
             for h in range(OUTPUT_BLOCKS):
-                nc.tensor.transpose(
-                    b_turned_psum[:, h * P : (h + 1) * P], b_rows[:, h, :], identity_bf16[:]
+                nc.tensor.transpose(bank[:, h * P : (h + 1) * P], b_rows[:, h, :], identity_bf16[:])
+            nc.scalar.mul(out=b_turned[:], in_=bank[:], mul=LORA_SCALE)
+
+        feature_order = "r (g p u e) -> r g u e p"
+
+        def build_w(g):
+            a_by_word = a_rows[:].rearrange(feature_order, g=PASSES, u=HALVES, e=PAIR)
+            for h in range(OUTPUT_BLOCKS):
+                w_by_word = w_rows[:, h, :].rearrange(feature_order, g=PASSES, u=HALVES, e=PAIR)
+                w_turned = sum_psum.tile([P, PACK * P], F32, tag="sum")
+                for u in range(HALVES):
+                    for e in range(PAIR):
+                        j = PAIR * u + e
+                        plane = w_turned[:, j * P : (j + 1) * P]
+                        nc.tensor.matmul(
+                            out=plane,
+                            lhsT=a_by_word[:, g, u, e, :],
+                            rhs=b_turned[:, h * P : (h + 1) * P],
+                            start=True,
+                            stop=False,
+                        )
+                        nc.tensor.matmul(
+                            out=plane,
+                            lhsT=w_by_word[:, g, u, e, :],
+                            rhs=identity_bf16[:],
+                            start=False,
+                            stop=True,
+                        )
+                nc.scalar.copy(
+                    out=w_grouped[:, g, h * P : (h + 1) * P, :],
+                    in_=w_turned[:].rearrange("p (j o) -> p o j", j=PACK),
                 )
-            nc.scalar.mul(out=b_turned[:], in_=b_turned_psum[:], mul=LORA_SCALE)
-            build_w(0)
-            prepare(LEAD - 1)
-            build_w(1)
 
-            bias_psum = sum_psum.tile([P, OUTPUTS], F32, tag="sum")
-            nc.tensor.matmul(
-                out=bias_psum[:], lhsT=ones[:], rhs=bias_row[:], start=True, stop=True
+        def quantise_w(g):
+            outputs = slice(g * OUTPUTS, (g + 1) * OUTPUTS)
+            nc.vector.quantize_mx(
+                out=w_codes[:, outputs].bitcast(FP8X4),
+                scales=w_scales[:, outputs],
+                in_=w_grouped[:, g, :, :].rearrange("p o j -> p (o j)"),
             )
-            nc.scalar.copy(out=bias[:], in_=bias_psum[:])
 
-            for b in range(1, BATCH):
-                turn_motion(b)
+        def spread_bias():
+            bank = sum_psum.tile([P, OUTPUTS], F32, tag="sum")
+            nc.tensor.matmul(out=bank[:], lhsT=ones[:], rhs=bias_row[:], start=True, stop=True)
+            nc.scalar.copy(out=bias[:], in_=bank[:])
 
-        result_pool = stack.enter_context(tc.tile_pool(name="result", bufs=3))
-
-        def multiply(c):
+        def multiply(c, i):
             codes, scales = packed[c]
-            sums = []
-            for i in range(CHUNK):
-                acc = sum_psum.tile([P, OUTPUTS], F32, tag="sum")
-                for g in range(PASSES):
-                    frames = slice((i * PASSES + g) * FRAMES, (i * PASSES + g + 1) * FRAMES)
-                    outputs = slice(g * OUTPUTS, (g + 1) * OUTPUTS)
-                    nc.tensor.matmul_mx(
-                        out=acc[:],
-                        lhsT=codes[:, frames].bitcast(FP8X4),
-                        lhsT_scale=scales[:, frames],
-                        rhs=w_codes[:, outputs].bitcast(FP8X4),
-                        rhs_scale=w_scales[:, outputs],
-                        start=(g == 0),
-                        stop=(g == PASSES - 1),
-                    )
-                sums.append(acc)
-            return sums
+            acc = sum_psum.tile([P, OUTPUTS], F32, tag="sum")
+            sums[c, i] = acc
+            for g in range(PASSES):
+                frames = slice((i * PASSES + g) * FRAMES, (i * PASSES + g + 1) * FRAMES)
+                outputs = slice(g * OUTPUTS, (g + 1) * OUTPUTS)
+                nc.tensor.matmul_mx(
+                    out=acc[:],
+                    lhsT=codes[:, frames].bitcast(FP8X4),
+                    lhsT_scale=scales[:, frames],
+                    rhs=w_codes[:, outputs].bitcast(FP8X4),
+                    rhs_scale=w_scales[:, outputs],
+                    start=(g == 0),
+                    stop=(g == PASSES - 1),
+                )
 
-        def finish(c, sums):
-            result = result_pool.tile([P, CHUNK, OUTPUTS], F32)
-            step = 1 if c == N_CHUNKS - 1 else CHUNK
+        def store(c, result, step):
+            for i in range(0, CHUNK, step):
+                nc.sync.dma_start(
+                    out=out[:, c * CHUNK + i : c * CHUNK + i + step, :],
+                    in_=result[:, i : i + step, :],
+                )
+
+        load_motion(0)
+        load_query(0, 1)
+        load_query(1, CHUNK // 2)
+        load_query(2, CHUNK)
+        nc.sync.dma_start(out=b_rows[:], in_=B_q.rearrange("(h o) r -> o h r", o=P))
+        nc.sync.dma_start(out=a_rows[:], in_=A_q)
+        nc.sync.dma_start(out=w_rows[:], in_=w_q.rearrange("(h o) k -> o h k", o=P))
+        nc.vector.memset(bias_row[:], 0.0)
+        nc.sync.dma_start(out=bias_row[0:1, :], in_=b_q.rearrange("(one o) -> one o", one=1))
+        load_motion(1)
+        for c in range(LEAD, LOAD_AHEAD):
+            load_query(c, CHUNK)
+        for b in range(2, BATCH):
+            load_motion(b)
+
+        make_identity(nc, identity_f32[:])
+        make_identity(nc, identity_bf16[:])
+        nc.vector.memset(ones[:], 1.0)
+
+        turn_motion(0)
+        for c in range(LEAD):
             for i in range(CHUNK):
-                if i < DETOUR:
-                    nc.scalar.copy(out=result[:, i, :], in_=sums[i][:])
-                    nc.gpsimd.tensor_tensor(
-                        out=result[:, i, :], in0=result[:, i, :], in1=bias[:], op=ADD
-                    )
-                else:
-                    nc.vector.tensor_tensor(
-                        out=result[:, i, :], in0=sums[i][:], in1=bias[:], op=ADD
-                    )
-                if (i + 1) % step == 0:
-                    nc.sync.dma_start(
-                        out=out[:, c * CHUNK + i + 1 - step : c * CHUNK + i + 1, :],
-                        in_=result[:, i + 1 - step : i + 1, :],
-                    )
+                turn(c, i)
+                add_motion(c, i)
+            if c > 0:
+                quantise(c - 1)
+        turn_lora()
+        build_w(0)
+        quantise_w(0)
+        build_w(1)
+        quantise_w(1)
+        turn_motion(1)
+        spread_bias()
+        sort_query(LEAD)
+        for i in range(CHUNK):
+            turn(LEAD, i)
+        sort_query(LEAD + 1)
 
         for c in range(N_CHUNKS):
-            ahead = c + LEAD
-            if ahead < N_CHUNKS:
-                banks = turn(ahead)
-            sums = multiply(c)
-            if ahead < N_CHUNKS:
-                grouped = add_motion(ahead, banks)
-            finish(c, sums)
-            if ahead < N_CHUNKS:
-                packed.append(quantise(grouped))
+            if c + LOAD_AHEAD < N_CHUNKS:
+                load_query(c + LOAD_AHEAD, CHUNK)
+            if c + LEAD - 1 < N_CHUNKS:
+                quantise(c + LEAD - 1)
+            for i in range(CHUNK):
+                multiply(c, i)
+            for i in range(CHUNK):
+                if c + LEAD < N_CHUNKS:
+                    add_motion(c + LEAD, i)
+                if c + LEAD + 1 < N_CHUNKS:
+                    turn(c + LEAD + 1, i)
+            result = result_pool.tile([P, CHUNK, OUTPUTS], F32)
+            for i in detour(c):
+                nc.scalar.copy(out=result[:, i, :], in_=sums[c, i][:])
+                nc.gpsimd.tensor_tensor(
+                    out=result[:, i, :], in0=result[:, i, :], in1=bias[:], op=ADD
+                )
+            if c + LEAD + 2 < N_CHUNKS:
+                sort_query(c + LEAD + 2)
+            for i in range(CHUNK):
+                if i not in detour(c):
+                    nc.vector.tensor_tensor(
+                        out=result[:, i, :], in0=sums[c, i][:], in1=bias[:], op=ADD
+                    )
+            for b in range(2, BATCH):
+                if c + LEAD + 2 == b * CHUNKS_PER_BATCH:
+                    turn_motion(b)
+            store(c, result, 1 if c == N_CHUNKS - 1 else CHUNK)

@@ -39,7 +39,7 @@ FLOPS = 2 * FRAMES * ROWS * FEATURES * OUTPUTS + 2 * OUTPUTS * RANK * FEATURES
 
 
 def detour(c):
-    return (2, 3) if c < N_CHUNKS - LEAD else ()
+    return (1, 3) if c < N_CHUNKS - LEAD else ()
 
 
 def tile_inversiontemporalmha_pa_t_kernel(tc, query, m, w_q, b_q, A_q, B_q, out):
@@ -268,26 +268,27 @@ def tile_inversiontemporalmha_pa_t_kernel(tc, query, m, w_q, b_q, A_q, B_q, out)
                 load_query(c + LOAD_AHEAD, CHUNK)
             if c + LEAD - 1 < N_CHUNKS:
                 quantise(c + LEAD - 1)
-            for i in range(CHUNK):
-                multiply(c, i)
-            for i in range(CHUNK):
-                if c + LEAD < N_CHUNKS:
-                    add_motion(c + LEAD, i)
-                if c + LEAD + 1 < N_CHUNKS:
-                    turn(c + LEAD + 1, i)
             result = result_pool.tile([P, CHUNK, OUTPUTS], F32)
-            for i in detour(c):
-                nc.scalar.copy(out=result[:, i, :], in_=sums[c, i][:])
-                nc.gpsimd.tensor_tensor(
-                    out=result[:, i, :], in0=result[:, i, :], in1=bias[:], op=ADD
-                )
-            if c + LEAD + 2 < N_CHUNKS:
-                sort_query(c + LEAD + 2)
-            for i in range(CHUNK):
-                if i not in detour(c):
-                    nc.vector.tensor_tensor(
-                        out=result[:, i, :], in0=sums[c, i][:], in1=bias[:], op=ADD
-                    )
+            for half in range(0, CHUNK, 2):
+                for i in (half, half + 1):
+                    multiply(c, i)
+                for i in (half, half + 1):
+                    if c + LEAD < N_CHUNKS:
+                        add_motion(c + LEAD, i)
+                    if c + LEAD + 1 < N_CHUNKS:
+                        turn(c + LEAD + 1, i)
+                for i in (half, half + 1):
+                    if i in detour(c):
+                        nc.scalar.copy(out=result[:, i, :], in_=sums[c, i][:])
+                        nc.gpsimd.tensor_tensor(
+                            out=result[:, i, :], in0=result[:, i, :], in1=bias[:], op=ADD
+                        )
+                    else:
+                        nc.vector.tensor_tensor(
+                            out=result[:, i, :], in0=sums[c, i][:], in1=bias[:], op=ADD
+                        )
+                if half == 0 and c + LEAD + 2 < N_CHUNKS:
+                    sort_query(c + LEAD + 2)
             for b in range(2, BATCH):
                 if c + LEAD + 2 == b * CHUNKS_PER_BATCH:
                     turn_motion(b)

@@ -31,15 +31,14 @@ OUTPUT_BLOCKS = OUTPUTS // P
 CHUNK = 4
 N_CHUNKS = ROWS // CHUNK
 CHUNKS_PER_BATCH = JOINTS // CHUNK
-LEAD = 3
-FIRST_SORTED = LEAD
-LOAD_AHEAD = 9
+LEAD = 5
+ROUND = 5
+N_ROUNDS = -(-ROWS // ROUND)
+DETOUR = 3
+UNSORTED = (0, 1, 3, 4)
+LOAD_AHEAD = 10
 
 FLOPS = 2 * FRAMES * ROWS * FEATURES * OUTPUTS + 2 * OUTPUTS * RANK * FEATURES
-
-
-def detour(c):
-    return (1, 3) if c < N_CHUNKS - LEAD else ()
 
 
 def tile_inversiontemporalmha_pa_t_kernel(tc, query, m, w_q, b_q, A_q, B_q, out):
@@ -49,7 +48,7 @@ def tile_inversiontemporalmha_pa_t_kernel(tc, query, m, w_q, b_q, A_q, B_q, out)
         q_pool = stack.enter_context(tc.tile_pool(name="q", bufs=LOAD_AHEAD))
         sorted_pool = stack.enter_context(tc.tile_pool(name="sorted", bufs=2))
         grouped_pool = stack.enter_context(tc.tile_pool(name="grouped", bufs=2))
-        packed_pool = stack.enter_context(tc.tile_pool(name="packed", bufs=LEAD + 1))
+        packed_pool = stack.enter_context(tc.tile_pool(name="packed", bufs=LEAD + 2))
         result_pool = stack.enter_context(tc.tile_pool(name="result", bufs=4))
         turn_psum = stack.enter_context(tc.psum_pool(name="turn_psum", bufs=CHUNK))
         sum_psum = stack.enter_context(tc.psum_pool(name="sum_psum", bufs=CHUNK))
@@ -71,7 +70,7 @@ def tile_inversiontemporalmha_pa_t_kernel(tc, query, m, w_q, b_q, A_q, B_q, out)
         b_turned = build.tile([P, OUTPUTS], BF16)
         w_grouped = build.tile([P, PASSES, OUTPUTS, PACK], BF16, align_bytes=64)
 
-        q_chunks, sorted_words, banks, grouped, packed, sums = {}, {}, {}, {}, {}, {}
+        q_chunks, sorted_words, banks, grouped, packed, results = {}, {}, {}, {}, {}, {}
 
         def load_motion(b):
             nc.sync.dma_start(out=m_rows[:, b, :], in_=m[b, :, :])
@@ -114,7 +113,7 @@ def tile_inversiontemporalmha_pa_t_kernel(tc, query, m, w_q, b_q, A_q, B_q, out)
         def turn(c, i):
             bank = turn_psum.tile([P, WORDS], F32, tag="turn")
             banks[c, i] = bank
-            if c < FIRST_SORTED:
+            if c in UNSORTED:
                 turn_rows(bank, every_second(q_chunks[c][:, i, :]))
             else:
                 words = sorted_words[c]
@@ -201,10 +200,13 @@ def tile_inversiontemporalmha_pa_t_kernel(tc, query, m, w_q, b_q, A_q, B_q, out)
             nc.tensor.matmul(out=bank[:], lhsT=ones[:], rhs=bias_row[:], start=True, stop=True)
             nc.scalar.copy(out=bias[:], in_=bank[:])
 
-        def multiply(c, i):
+        def multiply(n):
+            c, i = divmod(n, CHUNK)
             codes, scales = packed[c]
+            if i == 0:
+                result = result_pool.tile([P, CHUNK, OUTPUTS], F32)
+                results[c] = result
             acc = sum_psum.tile([P, OUTPUTS], F32, tag="sum")
-            sums[c, i] = acc
             for g in range(PASSES):
                 frames = slice((i * PASSES + g) * FRAMES, (i * PASSES + g + 1) * FRAMES)
                 outputs = slice(g * OUTPUTS, (g + 1) * OUTPUTS)
@@ -217,13 +219,16 @@ def tile_inversiontemporalmha_pa_t_kernel(tc, query, m, w_q, b_q, A_q, B_q, out)
                     start=(g == 0),
                     stop=(g == PASSES - 1),
                 )
+            return acc
 
-        def store(c, result, step):
-            for i in range(0, CHUNK, step):
-                nc.sync.dma_start(
-                    out=out[:, c * CHUNK + i : c * CHUNK + i + step, :],
-                    in_=result[:, i : i + step, :],
-                )
+        def result_of(n):
+            return results[n // CHUNK][:, n % CHUNK, :]
+
+        def store(n, tiles):
+            nc.sync.dma_start(
+                out=out[:, n + 1 - tiles : n + 1, :],
+                in_=results[n // CHUNK][:, n % CHUNK + 1 - tiles : n % CHUNK + 1, :],
+            )
 
         load_motion(0)
         load_query(0, 1)
@@ -235,7 +240,7 @@ def tile_inversiontemporalmha_pa_t_kernel(tc, query, m, w_q, b_q, A_q, B_q, out)
         nc.vector.memset(bias_row[:], 0.0)
         nc.sync.dma_start(out=bias_row[0:1, :], in_=b_q.rearrange("(one o) -> one o", one=1))
         load_motion(1)
-        for c in range(LEAD, LOAD_AHEAD):
+        for c in range(3, LOAD_AHEAD):
             load_query(c, CHUNK)
         for b in range(2, BATCH):
             load_motion(b)
@@ -244,52 +249,67 @@ def tile_inversiontemporalmha_pa_t_kernel(tc, query, m, w_q, b_q, A_q, B_q, out)
         make_identity(nc, identity_bf16[:])
         nc.vector.memset(ones[:], 1.0)
 
-        turn_motion(0)
-        for c in range(LEAD):
+        def prepare(c):
             for i in range(CHUNK):
                 turn(c, i)
                 add_motion(c, i)
-            if c > 0:
-                quantise(c - 1)
+
+        turn_motion(0)
+        prepare(0)
+        prepare(1)
+        quantise(0)
+        sort_query(2)
+        prepare(2)
+        quantise(1)
         turn_lora()
         build_w(0)
+        prepare(3)
         quantise_w(0)
+        quantise(2)
         build_w(1)
-        quantise_w(1)
         turn_motion(1)
-        spread_bias()
+        prepare(4)
+        quantise_w(1)
+        quantise(3)
         sort_query(LEAD)
+        spread_bias()
+        quantise(4)
         for i in range(CHUNK):
             turn(LEAD, i)
         sort_query(LEAD + 1)
 
-        for c in range(N_CHUNKS):
-            if c + LOAD_AHEAD < N_CHUNKS:
-                load_query(c + LOAD_AHEAD, CHUNK)
-            if c + LEAD - 1 < N_CHUNKS:
-                quantise(c + LEAD - 1)
-            result = result_pool.tile([P, CHUNK, OUTPUTS], F32)
-            for half in range(0, CHUNK, 2):
-                for i in (half, half + 1):
-                    multiply(c, i)
-                for i in (half, half + 1):
-                    if c + LEAD < N_CHUNKS:
-                        add_motion(c + LEAD, i)
-                    if c + LEAD + 1 < N_CHUNKS:
-                        turn(c + LEAD + 1, i)
-                for i in (half, half + 1):
-                    if i in detour(c):
-                        nc.scalar.copy(out=result[:, i, :], in_=sums[c, i][:])
-                        nc.gpsimd.tensor_tensor(
-                            out=result[:, i, :], in0=result[:, i, :], in1=bias[:], op=ADD
-                        )
-                    else:
-                        nc.vector.tensor_tensor(
-                            out=result[:, i, :], in0=sums[c, i][:], in1=bias[:], op=ADD
-                        )
-                if half == 0 and c + LEAD + 2 < N_CHUNKS:
-                    sort_query(c + LEAD + 2)
+        for r in range(N_ROUNDS):
+            c = r + LEAD
+            tiles = range(r * ROUND, min((r + 1) * ROUND, ROWS))
+            detour = tiles[:DETOUR] if c < N_CHUNKS else ()
+            sums = {}
+            if r + LOAD_AHEAD < N_CHUNKS:
+                load_query(r + LOAD_AHEAD, CHUNK)
+            for n in tiles:
+                sums[n] = multiply(n)
+                if n in detour:
+                    nc.scalar.copy(out=result_of(n), in_=sums[n][:])
+                    nc.gpsimd.tensor_tensor(
+                        out=result_of(n), in0=result_of(n), in1=bias[:], op=ADD
+                    )
+            if c + 2 < N_CHUNKS:
+                sort_query(c + 2)
+            for i in range(CHUNK):
+                if c < N_CHUNKS:
+                    add_motion(c, i)
+                if c + 1 < N_CHUNKS:
+                    turn(c + 1, i)
+            for n in tiles:
+                if n not in detour:
+                    nc.vector.tensor_tensor(
+                        out=result_of(n), in0=sums[n][:], in1=bias[:], op=ADD
+                    )
+                if n // CHUNK == N_CHUNKS - 1:
+                    store(n, 1)
+                elif n % CHUNK == CHUNK - 1:
+                    store(n, CHUNK)
+            if c < N_CHUNKS:
+                quantise(c)
             for b in range(2, BATCH):
-                if c + LEAD + 2 == b * CHUNKS_PER_BATCH:
+                if c + 2 == b * CHUNKS_PER_BATCH:
                     turn_motion(b)
-            store(c, result, 1 if c == N_CHUNKS - 1 else CHUNK)

@@ -34,7 +34,7 @@ CHUNKS_PER_BATCH = JOINTS // CHUNK
 LEAD = 5
 ROUND = 5
 N_ROUNDS = -(-ROWS // ROUND)
-DETOUR = 3
+DETOUR = 2
 UNSORTED = (0, 1, 3, 4)
 LOAD_AHEAD = 10
 

@@ -35,7 +35,7 @@ LEAD = 5
 ROUND = 5
 N_ROUNDS = -(-ROWS // ROUND)
 DETOUR = 2
-UNSORTED = (0, 1, 3, 4)
+TURNED_EVERY = 2
 LOAD_AHEAD = 10
 
 FLOPS = 2 * FRAMES * ROWS * FEATURES * OUTPUTS + 2 * OUTPUTS * RANK * FEATURES
@@ -53,15 +53,17 @@ def tile_inversiontemporalmha_pa_t_kernel(tc, query, m, w_q, b_q, A_q, B_q, out)
         turn_psum = stack.enter_context(tc.psum_pool(name="turn_psum", bufs=CHUNK))
         sum_psum = stack.enter_context(tc.psum_pool(name="sum_psum", bufs=CHUNK))
         build = stack.enter_context(tc.tile_pool(name="build", bufs=1))
+        flipped_pool = stack.enter_context(tc.tile_pool(name="flipped", bufs=2))
         stack.enter_context(tc.manual_schedule())
 
         identity_f32 = keep.tile([P, P], F32)
         identity_bf16 = keep.tile([P, P], BF16)
         ones = keep.tile([P, P], BF16)
-        m_turned = keep.tile([P, BATCH, WORDS], F32)
+        m_turned = keep.tile([P, BATCH - 1, WORDS], F32)
         w_codes = keep.tile([P, PASSES * OUTPUTS], U32, align_bytes=64)
         w_scales = keep.tile([P, PASSES * OUTPUTS], U8, align_bytes=64)
         bias = keep.tile([P, OUTPUTS], F32)
+        bias_columns = keep.tile([P, OUTPUT_BLOCKS, PAIR], F32)
         m_rows = build.tile([P, BATCH, FEATURES], BF16)
         b_rows = build.tile([P, OUTPUT_BLOCKS, RANK], BF16)
         a_rows = build.tile([P, FEATURES], BF16)
@@ -84,6 +86,13 @@ def tile_inversiontemporalmha_pa_t_kernel(tc, query, m, w_q, b_q, A_q, B_q, out)
                     in_=query[:, c * CHUNK + i : c * CHUNK + i + step, :],
                 )
 
+        def load_w(g):
+            features = slice(g * PACK * P, (g + 1) * PACK * P)
+            nc.sync.dma_start(
+                out=w_rows[:, :, features],
+                in_=w_q[:, features].rearrange("(h o) k -> o h k", o=P),
+            )
+
         def sort_query(c):
             words = sorted_pool.tile([P, HALVES, CHUNK * HALF], F32, tag="sorted")
             sorted_words[c] = words
@@ -96,6 +105,20 @@ def tile_inversiontemporalmha_pa_t_kernel(tc, query, m, w_q, b_q, A_q, B_q, out)
                         "p (n u) -> p u n", u=HALVES
                     ),
                 )
+
+        def add_early(c, i):
+            if i == 0:
+                words = sorted_pool.tile([P, HALVES, CHUNK * HALF], F32, tag="sorted")
+                sorted_words[c] = words
+            b = c // CHUNKS_PER_BATCH
+            nc.vector.tensor_tensor(
+                out=sorted_words[c][:, :, i * HALF : (i + 1) * HALF]
+                .bitcast(BF16)
+                .rearrange("p u (n e) -> p u n e", e=PAIR),
+                in0=q_chunks[c][:, i, :].rearrange("p (n u e) -> p u n e", u=HALVES, e=PAIR),
+                in1=m_rows[:, b, :].rearrange("p (n u e) -> p u n e", u=HALVES, e=PAIR),
+                op=ADD,
+            )
 
         def turn_rows(bank, words_of):
             for u in range(HALVES):
@@ -113,7 +136,7 @@ def tile_inversiontemporalmha_pa_t_kernel(tc, query, m, w_q, b_q, A_q, B_q, out)
         def turn(c, i):
             bank = turn_psum.tile([P, WORDS], F32, tag="turn")
             banks[c, i] = bank
-            if c in UNSORTED:
+            if c == LEAD:
                 turn_rows(bank, every_second(q_chunks[c][:, i, :]))
             else:
                 words = sorted_words[c]
@@ -125,8 +148,17 @@ def tile_inversiontemporalmha_pa_t_kernel(tc, query, m, w_q, b_q, A_q, B_q, out)
             bank = sum_psum.tile([P, WORDS], F32, tag="sum")
             turn_rows(bank, every_second(m_rows[:, b, :]))
             nc.scalar.copy(
-                out=m_turned[:, b, :].rearrange("p (x u) -> p x u", u=HALVES),
+                out=m_turned[:, b - 1, :].rearrange("p (x u) -> p x u", u=HALVES),
                 in_=bank[:].rearrange("p (u x) -> p x u", u=HALVES),
+            )
+
+        def group_early(c, i):
+            if i == 0:
+                pairs = grouped_pool.tile([P, CHUNK, FEATURES], BF16, align_bytes=64)
+                grouped[c] = pairs
+            nc.scalar.copy(
+                out=grouped[c][:, i, :].bitcast(F32).rearrange("p (x u) -> p x u", u=HALVES),
+                in_=banks[c, i][:].rearrange("p (u x) -> p x u", u=HALVES),
             )
 
         def add_motion(c, i):
@@ -137,7 +169,7 @@ def tile_inversiontemporalmha_pa_t_kernel(tc, query, m, w_q, b_q, A_q, B_q, out)
             nc.vector.tensor_tensor(
                 out=grouped[c][:, i, :].rearrange("p (x u e) -> p x u e", u=HALVES, e=PAIR),
                 in0=banks[c, i][:].bitcast(BF16).rearrange("p (u x e) -> p x u e", u=HALVES, e=PAIR),
-                in1=m_turned[:, b, :].bitcast(BF16).rearrange("p (x u e) -> p x u e", u=HALVES, e=PAIR),
+                in1=m_turned[:, b - 1, :].bitcast(BF16).rearrange("p (x u e) -> p x u e", u=HALVES, e=PAIR),
                 op=ADD,
             )
 
@@ -199,14 +231,27 @@ def tile_inversiontemporalmha_pa_t_kernel(tc, query, m, w_q, b_q, A_q, B_q, out)
             bank = sum_psum.tile([P, OUTPUTS], F32, tag="sum")
             nc.tensor.matmul(out=bank[:], lhsT=ones[:], rhs=bias_row[:], start=True, stop=True)
             nc.scalar.copy(out=bias[:], in_=bank[:])
+            columns = sum_psum.tile([P, OUTPUT_BLOCKS, PAIR], F32, tag="sum")
+            for h in range(OUTPUT_BLOCKS):
+                nc.tensor.matmul(
+                    out=columns[:, h, :],
+                    lhsT=bias_row[:, h * P : (h + 1) * P],
+                    rhs=ones[:, :PAIR],
+                    start=True,
+                    stop=True,
+                )
+            nc.scalar.copy(out=bias_columns[:], in_=columns[:])
 
-        def multiply(n):
+        def multiply(n, spare):
             c, i = divmod(n, CHUNK)
             codes, scales = packed[c]
             if i == 0:
                 result = result_pool.tile([P, CHUNK, OUTPUTS], F32)
                 results[c] = result
-            acc = sum_psum.tile([P, OUTPUTS], F32, tag="sum")
+            if spare:
+                acc = turn_psum.tile([P, OUTPUTS], F32, tag="turn")
+            else:
+                acc = sum_psum.tile([P, OUTPUTS], F32, tag="sum")
             for g in range(PASSES):
                 frames = slice((i * PASSES + g) * FRAMES, (i * PASSES + g + 1) * FRAMES)
                 outputs = slice(g * OUTPUTS, (g + 1) * OUTPUTS)
@@ -220,6 +265,44 @@ def tile_inversiontemporalmha_pa_t_kernel(tc, query, m, w_q, b_q, A_q, B_q, out)
                     stop=(g == PASSES - 1),
                 )
             return acc
+
+        def multiply_turned(n):
+            c, i = divmod(n, CHUNK)
+            codes, scales = packed[c]
+            if i == 0:
+                result = result_pool.tile([P, CHUNK, OUTPUTS], F32)
+                results[c] = result
+            acc = sum_psum.tile([P, OUTPUTS], F32, tag="sum")
+            for h in range(OUTPUT_BLOCKS):
+                for g in range(PASSES):
+                    frames = slice((i * PASSES + g) * FRAMES, (i * PASSES + g + 1) * FRAMES)
+                    outputs = slice(g * OUTPUTS + h * P, g * OUTPUTS + (h + 1) * P)
+                    nc.tensor.matmul_mx(
+                        out=acc[:, h * P : (h + 1) * P],
+                        lhsT=w_codes[:, outputs].bitcast(FP8X4),
+                        lhsT_scale=w_scales[:, outputs],
+                        rhs=codes[:, frames].bitcast(FP8X4),
+                        rhs_scale=scales[:, frames],
+                        start=(g == 0),
+                        stop=(g == PASSES - 1),
+                    )
+            flipped = flipped_pool.tile([P, OUTPUTS], F32)
+            for h in range(OUTPUT_BLOCKS):
+                nc.scalar.activation(
+                    out=flipped[:, h * P : (h + 1) * P],
+                    in_=acc[:, h * P : (h + 1) * P],
+                    func=mybir.ActivationFunctionType.Identity,
+                    bias=bias_columns[:, h, 0:1],
+                    scale=1.0,
+                )
+            return flipped
+
+        def turn_back(n, flipped):
+            bank = sum_psum.tile([P, OUTPUTS], F32, tag="sum")
+            for h in range(OUTPUT_BLOCKS):
+                block = slice(h * P, (h + 1) * P)
+                nc.tensor.transpose(bank[:, block], flipped[:, block], identity_f32[:])
+            nc.scalar.copy(out=result_of(n), in_=bank[:])
 
         def result_of(n):
             return results[n // CHUNK][:, n % CHUNK, :]
@@ -236,11 +319,14 @@ def tile_inversiontemporalmha_pa_t_kernel(tc, query, m, w_q, b_q, A_q, B_q, out)
         load_query(2, CHUNK)
         nc.sync.dma_start(out=b_rows[:], in_=B_q.rearrange("(h o) r -> o h r", o=P))
         nc.sync.dma_start(out=a_rows[:], in_=A_q)
-        nc.sync.dma_start(out=w_rows[:], in_=w_q.rearrange("(h o) k -> o h k", o=P))
+        load_w(0)
+        load_query(3, CHUNK)
+        load_w(1)
+        load_motion(1)
+        load_query(4, CHUNK)
         nc.vector.memset(bias_row[:], 0.0)
         nc.sync.dma_start(out=bias_row[0:1, :], in_=b_q.rearrange("(one o) -> one o", one=1))
-        load_motion(1)
-        for c in range(3, LOAD_AHEAD):
+        for c in range(LEAD, LOAD_AHEAD):
             load_query(c, CHUNK)
         for b in range(2, BATCH):
             load_motion(b)
@@ -249,44 +335,50 @@ def tile_inversiontemporalmha_pa_t_kernel(tc, query, m, w_q, b_q, A_q, B_q, out)
         make_identity(nc, identity_bf16[:])
         nc.vector.memset(ones[:], 1.0)
 
-        def prepare(c):
+        def prepare_early(c):
+            for i in range(CHUNK):
+                add_early(c, i)
             for i in range(CHUNK):
                 turn(c, i)
-                add_motion(c, i)
+                group_early(c, i)
 
-        turn_motion(0)
-        prepare(0)
-        prepare(1)
+        prepare_early(0)
+        prepare_early(1)
         quantise(0)
-        sort_query(2)
-        prepare(2)
+        prepare_early(2)
         quantise(1)
         turn_lora()
         build_w(0)
-        prepare(3)
-        quantise_w(0)
+        prepare_early(3)
         quantise(2)
+        quantise_w(0)
         build_w(1)
         turn_motion(1)
-        prepare(4)
-        quantise_w(1)
+        for i in range(CHUNK):
+            add_early(4, i)
         quantise(3)
-        sort_query(LEAD)
-        spread_bias()
-        quantise(4)
+        quantise_w(1)
+        for i in range(CHUNK):
+            turn(4, i)
+            group_early(4, i)
         for i in range(CHUNK):
             turn(LEAD, i)
+        spread_bias()
         sort_query(LEAD + 1)
 
         for r in range(N_ROUNDS):
             c = r + LEAD
             tiles = range(r * ROUND, min((r + 1) * ROUND, ROWS))
-            detour = tiles[:DETOUR] if c < N_CHUNKS else ()
+            ahead = c < N_CHUNKS
+            turned = tiles[:1] if ahead and r % TURNED_EVERY == 1 else ()
+            detour = tiles[len(turned) : len(turned) + DETOUR] if r < N_ROUNDS - 1 else ()
             sums = {}
             if r + LOAD_AHEAD < N_CHUNKS:
                 load_query(r + LOAD_AHEAD, CHUNK)
-            for n in tiles:
-                sums[n] = multiply(n)
+            for n in turned:
+                flipped = multiply_turned(n)
+            for n in tiles[len(turned) :]:
+                sums[n] = multiply(n, c == N_CHUNKS and n in tiles[:CHUNK])
                 if n in detour:
                     nc.scalar.copy(out=result_of(n), in_=sums[n][:])
                     nc.gpsimd.tensor_tensor(
@@ -299,8 +391,12 @@ def tile_inversiontemporalmha_pa_t_kernel(tc, query, m, w_q, b_q, A_q, B_q, out)
                     add_motion(c, i)
                 if c + 1 < N_CHUNKS:
                     turn(c + 1, i)
+            for n in turned:
+                turn_back(n, flipped)
+            if r == 0:
+                quantise(LEAD - 1)
             for n in tiles:
-                if n not in detour:
+                if n not in detour and n not in turned:
                     nc.vector.tensor_tensor(
                         out=result_of(n), in0=sums[n][:], in1=bias[:], op=ADD
                     )

@@ -67,7 +67,10 @@ def tile_inversiontemporalmha_pa_t_kernel(tc, query, m, w_q, b_q, A_q, B_q, out)
         m_rows = build.tile([P, BATCH, FEATURES], BF16)
         b_rows = build.tile([P, OUTPUT_BLOCKS, RANK], BF16)
         a_rows = build.tile([P, FEATURES], BF16)
-        w_rows = build.tile([P, OUTPUT_BLOCKS, FEATURES], BF16)
+        w_rows = []
+        for g in range(PASSES):
+            w_rows_g = build.tile([P, OUTPUT_BLOCKS, PACK * P], BF16, tag=f"w_rows_{g}")
+            w_rows.append(w_rows_g)
         bias_row = build.tile([P, OUTPUTS], BF16)
         b_turned = build.tile([P, OUTPUTS], BF16)
         w_grouped = build.tile([P, PASSES, OUTPUTS, PACK], BF16, align_bytes=64)
@@ -89,7 +92,7 @@ def tile_inversiontemporalmha_pa_t_kernel(tc, query, m, w_q, b_q, A_q, B_q, out)
         def load_w(g):
             features = slice(g * PACK * P, (g + 1) * PACK * P)
             nc.sync.dma_start(
-                out=w_rows[:, :, features],
+                out=w_rows[g][:],
                 in_=w_q[:, features].rearrange("(h o) k -> o h k", o=P),
             )
 
@@ -189,12 +192,12 @@ def tile_inversiontemporalmha_pa_t_kernel(tc, query, m, w_q, b_q, A_q, B_q, out)
                 nc.tensor.transpose(bank[:, h * P : (h + 1) * P], b_rows[:, h, :], identity_bf16[:])
             nc.scalar.mul(out=b_turned[:], in_=bank[:], mul=LORA_SCALE)
 
-        feature_order = "r (g p u e) -> r g u e p"
-
         def build_w(g):
-            a_by_word = a_rows[:].rearrange(feature_order, g=PASSES, u=HALVES, e=PAIR)
+            a_by_word = a_rows[:].rearrange(
+                "r (g p u e) -> r g u e p", g=PASSES, u=HALVES, e=PAIR
+            )
             for h in range(OUTPUT_BLOCKS):
-                w_by_word = w_rows[:, h, :].rearrange(feature_order, g=PASSES, u=HALVES, e=PAIR)
+                w_by_word = w_rows[g][:, h, :].rearrange("o (p u e) -> o u e p", u=HALVES, e=PAIR)
                 w_turned = sum_psum.tile([P, PACK * P], F32, tag="sum")
                 for u in range(HALVES):
                     for e in range(PAIR):
@@ -209,7 +212,7 @@ def tile_inversiontemporalmha_pa_t_kernel(tc, query, m, w_q, b_q, A_q, B_q, out)
                         )
                         nc.tensor.matmul(
                             out=plane,
-                            lhsT=w_by_word[:, g, u, e, :],
+                            lhsT=w_by_word[:, u, e, :],
                             rhs=identity_bf16[:],
                             start=False,
                             stop=True,
@@ -335,50 +338,54 @@ def tile_inversiontemporalmha_pa_t_kernel(tc, query, m, w_q, b_q, A_q, B_q, out)
         make_identity(nc, identity_bf16[:])
         nc.vector.memset(ones[:], 1.0)
 
-        def prepare_early(c):
+        def add_chunk(c):
             for i in range(CHUNK):
                 add_early(c, i)
+
+        def turn_chunk(c):
             for i in range(CHUNK):
                 turn(c, i)
                 group_early(c, i)
 
-        prepare_early(0)
-        prepare_early(1)
+        add_chunk(0)
+        turn_chunk(0)
+        add_chunk(1)
+        turn_chunk(1)
         quantise(0)
-        prepare_early(2)
-        quantise(1)
+        add_chunk(2)
         turn_lora()
+        turn_chunk(2)
+        quantise(1)
         build_w(0)
-        prepare_early(3)
+        add_chunk(3)
+        turn_chunk(3)
         quantise(2)
         quantise_w(0)
         build_w(1)
-        turn_motion(1)
-        for i in range(CHUNK):
-            add_early(4, i)
+        add_chunk(4)
         quantise(3)
+        turn_chunk(4)
+        turn_motion(1)
         quantise_w(1)
         for i in range(CHUNK):
-            turn(4, i)
-            group_early(4, i)
-        for i in range(CHUNK):
             turn(LEAD, i)
-        spread_bias()
         sort_query(LEAD + 1)
+        spread_bias()
 
         for r in range(N_ROUNDS):
             c = r + LEAD
             tiles = range(r * ROUND, min((r + 1) * ROUND, ROWS))
             ahead = c < N_CHUNKS
-            turned = tiles[:1] if ahead and r % TURNED_EVERY == 1 else ()
-            detour = tiles[len(turned) : len(turned) + DETOUR] if r < N_ROUNDS - 1 else ()
+            detour = tiles[:DETOUR] if r < N_ROUNDS - 1 else ()
+            turned = tiles[DETOUR : DETOUR + 1] if ahead and r % TURNED_EVERY == 1 else ()
             sums = {}
             if r + LOAD_AHEAD < N_CHUNKS:
                 load_query(r + LOAD_AHEAD, CHUNK)
-            for n in turned:
-                flipped = multiply_turned(n)
-            for n in tiles[len(turned) :]:
-                sums[n] = multiply(n, c == N_CHUNKS and n in tiles[:CHUNK])
+            for n in tiles:
+                if n in turned:
+                    flipped = multiply_turned(n)
+                else:
+                    sums[n] = multiply(n, c == N_CHUNKS and n in tiles[:CHUNK])
                 if n in detour:
                     nc.scalar.copy(out=result_of(n), in_=sums[n][:])
                     nc.gpsimd.tensor_tensor(

@@ -36,6 +36,7 @@ ROUND = 5
 N_ROUNDS = -(-ROWS // ROUND)
 DETOUR = 2
 TURNED_EVERY = 2
+LAST_CHUNKS = 6
 LOAD_AHEAD = 10
 
 FLOPS = 2 * FRAMES * ROWS * FEATURES * OUTPUTS + 2 * OUTPUTS * RANK * FEATURES
@@ -376,8 +377,8 @@ def tile_inversiontemporalmha_pa_t_kernel(tc, query, m, w_q, b_q, A_q, B_q, out)
             c = r + LEAD
             tiles = range(r * ROUND, min((r + 1) * ROUND, ROWS))
             ahead = c < N_CHUNKS
-            detour = tiles[:DETOUR] if r < N_ROUNDS - 1 else ()
-            turned = tiles[DETOUR : DETOUR + 1] if ahead and r % TURNED_EVERY == 1 else ()
+            turned = tiles[1:2] if ahead and r % TURNED_EVERY == 1 else ()
+            detour = [n for n in tiles if n not in turned][:DETOUR] if r < N_ROUNDS - 1 else ()
             sums = {}
             if r + LOAD_AHEAD < N_CHUNKS:
                 load_query(r + LOAD_AHEAD, CHUNK)
@@ -393,13 +394,13 @@ def tile_inversiontemporalmha_pa_t_kernel(tc, query, m, w_q, b_q, A_q, B_q, out)
                     )
             if c + 2 < N_CHUNKS:
                 sort_query(c + 2)
+            for n in turned:
+                turn_back(n, flipped)
             for i in range(CHUNK):
                 if c < N_CHUNKS:
                     add_motion(c, i)
                 if c + 1 < N_CHUNKS:
                     turn(c + 1, i)
-            for n in turned:
-                turn_back(n, flipped)
             if r == 0:
                 quantise(LEAD - 1)
             for n in tiles:
@@ -407,7 +408,7 @@ def tile_inversiontemporalmha_pa_t_kernel(tc, query, m, w_q, b_q, A_q, B_q, out)
                     nc.vector.tensor_tensor(
                         out=result_of(n), in0=sums[n][:], in1=bias[:], op=ADD
                     )
-                if n // CHUNK == N_CHUNKS - 1:
+                if n // CHUNK >= N_CHUNKS - LAST_CHUNKS:
                     store(n, 1)
                 elif n % CHUNK == CHUNK - 1:
                     store(n, CHUNK)

from contextlib import ExitStack

import concourse.mybir as mybir
from concourse.masks import make_identity

BF16 = mybir.dt.bfloat16
F32 = mybir.dt.float32
U32 = mybir.dt.uint32
U8 = mybir.dt.uint8
FP8X4 = mybir.dt.float8_e4m3fn_x4
ADD = mybir.AluOpType.add

P = 128
FRAMES = 128
BATCH = 4
JOINTS = 16
ROWS = BATCH * JOINTS
FEATURES = 1024
OUTPUTS = 512
RANK = 128
LORA_SCALE = 2.0

PACK = 4
PASSES = FEATURES // (P * PACK)
WORDS = FEATURES // 2
PAIR = 2
HALVES = 2
HALF = WORDS // HALVES
OUTPUT_BLOCKS = OUTPUTS // P

CHUNK = 4
N_CHUNKS = ROWS // CHUNK
CHUNKS_PER_BATCH = JOINTS // CHUNK
LEAD = 5
ROUND = 5
N_ROUNDS = -(-ROWS // ROUND)
DETOUR = 2
TURNED_EVERY = 2
LAST_CHUNKS = 6
LOAD_AHEAD = 10

FLOPS = 2 * FRAMES * ROWS * FEATURES * OUTPUTS + 2 * OUTPUTS * RANK * FEATURES


def tile_inversiontemporalmha_pa_t_kernel(tc, query, m, w_q, b_q, A_q, B_q, out):
    nc = tc.nc
    with ExitStack() as stack:
        keep = stack.enter_context(tc.tile_pool(name="keep", bufs=1))
        q_pool = stack.enter_context(tc.tile_pool(name="q", bufs=LOAD_AHEAD))
        sorted_pool = stack.enter_context(tc.tile_pool(name="sorted", bufs=2))
        grouped_pool = stack.enter_context(tc.tile_pool(name="grouped", bufs=2))
        packed_pool = stack.enter_context(tc.tile_pool(name="packed", bufs=LEAD + 2))
        result_pool = stack.enter_context(tc.tile_pool(name="result", bufs=4))
        turn_psum = stack.enter_context(tc.psum_pool(name="turn_psum", bufs=CHUNK))
        sum_psum = stack.enter_context(tc.psum_pool(name="sum_psum", bufs=CHUNK))
        build = stack.enter_context(tc.tile_pool(name="build", bufs=1))
        flipped_pool = stack.enter_context(tc.tile_pool(name="flipped", bufs=2))
        stack.enter_context(tc.manual_schedule())

        identity_f32 = keep.tile([P, P], F32)
        identity_bf16 = keep.tile([P, P], BF16)
        ones = keep.tile([P, P], BF16)
        m_turned = keep.tile([P, BATCH - 1, WORDS], F32)
        w_codes = keep.tile([P, PASSES * OUTPUTS], U32, align_bytes=64)
        w_scales = keep.tile([P, PASSES * OUTPUTS], U8, align_bytes=64)
        bias = keep.tile([P, OUTPUTS], F32)
        bias_columns = keep.tile([P, OUTPUT_BLOCKS, PAIR], F32)
        m_rows = build.tile([P, BATCH, FEATURES], BF16)
        b_rows = build.tile([P, OUTPUT_BLOCKS, RANK], BF16)
        a_rows = build.tile([P, FEATURES], BF16)
        w_rows = []
        for g in range(PASSES):
            w_rows_g = build.tile([P, OUTPUT_BLOCKS, PACK * P], BF16, tag=f"w_rows_{g}")
            w_rows.append(w_rows_g)
        bias_row = build.tile([P, OUTPUTS], BF16)
        b_turned = build.tile([P, OUTPUTS], BF16)
        w_grouped = build.tile([P, PASSES, OUTPUTS, PACK], BF16, align_bytes=64)

        q_chunks, sorted_words, banks, grouped, packed, results = {}, {}, {}, {}, {}, {}

        def load_motion(b):
            nc.sync.dma_start(out=m_rows[:, b, :], in_=m[b, :, :])

        def load_query(c, step):
            q_rows = q_pool.tile([P, CHUNK, FEATURES], BF16)
            q_chunks[c] = q_rows
            for i in range(0, CHUNK, step):
                nc.sync.dma_start(
                    out=q_rows[:, i : i + step, :],
                    in_=query[:, c * CHUNK + i : c * CHUNK + i + step, :],
                )

        def load_w(g):
            features = slice(g * PACK * P, (g + 1) * PACK * P)
            nc.sync.dma_start(
                out=w_rows[g][:],
                in_=w_q[:, features].rearrange("(h o) k -> o h k", o=P),
            )

        def sort_query(c):
            words = sorted_pool.tile([P, HALVES, CHUNK * HALF], F32, tag="sorted")
            sorted_words[c] = words
            rows = q_chunks[c][:].rearrange("p i k -> p (i k)").bitcast(F32)
            step = CHUNK // 2
            for i in range(0, CHUNK, step):
                nc.scalar.copy(
                    out=words[:, :, i * HALF : (i + step) * HALF],
                    in_=rows[:, i * WORDS : (i + step) * WORDS].rearrange(
                        "p (n u) -> p u n", u=HALVES
                    ),
                )

        def add_early(c, i):
            if i == 0:
                words = sorted_pool.tile([P, HALVES, CHUNK * HALF], F32, tag="sorted")
                sorted_words[c] = words
            b = c // CHUNKS_PER_BATCH
            nc.vector.tensor_tensor(
                out=sorted_words[c][:, :, i * HALF : (i + 1) * HALF]
                .bitcast(BF16)
                .rearrange("p u (n e) -> p u n e", e=PAIR),
                in0=q_chunks[c][:, i, :].rearrange("p (n u e) -> p u n e", u=HALVES, e=PAIR),
                in1=m_rows[:, b, :].rearrange("p (n u e) -> p u n e", u=HALVES, e=PAIR),
                op=ADD,
            )

        def turn_rows(bank, words_of):
            for u in range(HALVES):
                for g in range(PASSES):
                    nc.tensor.transpose(
                        bank[:, (u * PASSES + g) * P : (u * PASSES + g + 1) * P],
                        words_of(u, g),
                        identity_f32[:],
                    )

        def every_second(row):
            words = row.bitcast(F32)
            return lambda u, g: words[:, g * HALVES * P + u : (g + 1) * HALVES * P : HALVES]

        def turn(c, i):
            bank = turn_psum.tile([P, WORDS], F32, tag="turn")
            banks[c, i] = bank
            if c == LEAD:
                turn_rows(bank, every_second(q_chunks[c][:, i, :]))
            else:
                words = sorted_words[c]
                turn_rows(
                    bank, lambda u, g: words[:, u, i * HALF + g * P : i * HALF + (g + 1) * P]
                )

        def turn_motion(b):
            bank = sum_psum.tile([P, WORDS], F32, tag="sum")
            turn_rows(bank, every_second(m_rows[:, b, :]))
            nc.scalar.copy(
                out=m_turned[:, b - 1, :].rearrange("p (x u) -> p x u", u=HALVES),
                in_=bank[:].rearrange("p (u x) -> p x u", u=HALVES),
            )

        def group_early(c, i):
            if i == 0:
                pairs = grouped_pool.tile([P, CHUNK, FEATURES], BF16, align_bytes=64)
                grouped[c] = pairs
            nc.scalar.copy(
                out=grouped[c][:, i, :].bitcast(F32).rearrange("p (x u) -> p x u", u=HALVES),
                in_=banks[c, i][:].rearrange("p (u x) -> p x u", u=HALVES),
            )

        def add_motion(c, i):
            if i == 0:
                pairs = grouped_pool.tile([P, CHUNK, FEATURES], BF16, align_bytes=64)
                grouped[c] = pairs
            b = c // CHUNKS_PER_BATCH
            nc.vector.tensor_tensor(
                out=grouped[c][:, i, :].rearrange("p (x u e) -> p x u e", u=HALVES, e=PAIR),
                in0=banks[c, i][:].bitcast(BF16).rearrange("p (u x e) -> p x u e", u=HALVES, e=PAIR),
                in1=m_turned[:, b - 1, :].bitcast(BF16).rearrange("p (x u e) -> p x u e", u=HALVES, e=PAIR),
                op=ADD,
            )

        def quantise(c):
            codes = packed_pool.tile([P, CHUNK * PASSES * FRAMES], U32, align_bytes=64)
            scales = packed_pool.tile([P, CHUNK * PASSES * FRAMES], U8, align_bytes=64)
            packed[c] = (codes, scales)
            nc.vector.quantize_mx(
                out=codes[:].bitcast(FP8X4),
                scales=scales[:],
                in_=grouped[c][:].rearrange("p i n -> p (i n)"),
            )

        def turn_lora():
            bank = sum_psum.tile([P, OUTPUTS], BF16, tag="sum")
            for h in range(OUTPUT_BLOCKS):
                nc.tensor.transpose(bank[:, h * P : (h + 1) * P], b_rows[:, h, :], identity_bf16[:])
            nc.scalar.mul(out=b_turned[:], in_=bank[:], mul=LORA_SCALE)

        def build_w(g):
            a_by_word = a_rows[:].rearrange(
                "r (g p u e) -> r g u e p", g=PASSES, u=HALVES, e=PAIR
            )
            for h in range(OUTPUT_BLOCKS):
                w_by_word = w_rows[g][:, h, :].rearrange("o (p u e) -> o u e p", u=HALVES, e=PAIR)
                w_turned = sum_psum.tile([P, PACK * P], F32, tag="sum")
                for u in range(HALVES):
                    for e in range(PAIR):
                        j = PAIR * u + e
                        plane = w_turned[:, j * P : (j + 1) * P]
                        nc.tensor.matmul(
                            out=plane,
                            lhsT=a_by_word[:, g, u, e, :],
                            rhs=b_turned[:, h * P : (h + 1) * P],
                            start=True,
                            stop=False,
                        )
                        nc.tensor.matmul(
                            out=plane,
                            lhsT=w_by_word[:, u, e, :],
                            rhs=identity_bf16[:],
                            start=False,
                            stop=True,
                        )
                nc.scalar.copy(
                    out=w_grouped[:, g, h * P : (h + 1) * P, :],
                    in_=w_turned[:].rearrange("p (j o) -> p o j", j=PACK),
                )

        def quantise_w(g):
            outputs = slice(g * OUTPUTS, (g + 1) * OUTPUTS)
            nc.vector.quantize_mx(
                out=w_codes[:, outputs].bitcast(FP8X4),
                scales=w_scales[:, outputs],
                in_=w_grouped[:, g, :, :].rearrange("p o j -> p (o j)"),
            )

        def spread_bias():
            bank = sum_psum.tile([P, OUTPUTS], F32, tag="sum")
            nc.tensor.matmul(out=bank[:], lhsT=ones[:], rhs=bias_row[:], start=True, stop=True)
            nc.scalar.copy(out=bias[:], in_=bank[:])
            columns = sum_psum.tile([P, OUTPUT_BLOCKS, PAIR], F32, tag="sum")
            for h in range(OUTPUT_BLOCKS):
                nc.tensor.matmul(
                    out=columns[:, h, :],
                    lhsT=bias_row[:, h * P : (h + 1) * P],
                    rhs=ones[:, :PAIR],
                    start=True,
                    stop=True,
                )
            nc.scalar.copy(out=bias_columns[:], in_=columns[:])

        def multiply(n, spare):
            c, i = divmod(n, CHUNK)
            codes, scales = packed[c]
            if i == 0:
                result = result_pool.tile([P, CHUNK, OUTPUTS], F32)
                results[c] = result
            if spare:
                acc = turn_psum.tile([P, OUTPUTS], F32, tag="turn")
            else:
                acc = sum_psum.tile([P, OUTPUTS], F32, tag="sum")
            for g in range(PASSES):
                frames = slice((i * PASSES + g) * FRAMES, (i * PASSES + g + 1) * FRAMES)
                outputs = slice(g * OUTPUTS, (g + 1) * OUTPUTS)
                nc.tensor.matmul_mx(
                    out=acc[:],
                    lhsT=codes[:, frames].bitcast(FP8X4),
                    lhsT_scale=scales[:, frames],
                    rhs=w_codes[:, outputs].bitcast(FP8X4),
                    rhs_scale=w_scales[:, outputs],
                    start=(g == 0),
                    stop=(g == PASSES - 1),
                )
            return acc

        def multiply_turned(n):
            c, i = divmod(n, CHUNK)
            codes, scales = packed[c]
            if i == 0:
                result = result_pool.tile([P, CHUNK, OUTPUTS], F32)
                results[c] = result
            acc = sum_psum.tile([P, OUTPUTS], F32, tag="sum")
            for h in range(OUTPUT_BLOCKS):
                for g in range(PASSES):
                    frames = slice((i * PASSES + g) * FRAMES, (i * PASSES + g + 1) * FRAMES)
                    outputs = slice(g * OUTPUTS + h * P, g * OUTPUTS + (h + 1) * P)
                    nc.tensor.matmul_mx(
                        out=acc[:, h * P : (h + 1) * P],
                        lhsT=w_codes[:, outputs].bitcast(FP8X4),
                        lhsT_scale=w_scales[:, outputs],
                        rhs=codes[:, frames].bitcast(FP8X4),
                        rhs_scale=scales[:, frames],
                        start=(g == 0),
                        stop=(g == PASSES - 1),
                    )
            flipped = flipped_pool.tile([P, OUTPUTS], F32)
            for h in range(OUTPUT_BLOCKS):
                nc.scalar.activation(
                    out=flipped[:, h * P : (h + 1) * P],
                    in_=acc[:, h * P : (h + 1) * P],
                    func=mybir.ActivationFunctionType.Identity,
                    bias=bias_columns[:, h, 0:1],
                    scale=1.0,
                )
            return flipped

        def turn_back(n, flipped):
            bank = sum_psum.tile([P, OUTPUTS], F32, tag="sum")
            for h in range(OUTPUT_BLOCKS):
                block = slice(h * P, (h + 1) * P)
                nc.tensor.transpose(bank[:, block], flipped[:, block], identity_f32[:])
            nc.scalar.copy(out=result_of(n), in_=bank[:])

        def result_of(n):
            return results[n // CHUNK][:, n % CHUNK, :]

        def store(n, tiles):
            nc.sync.dma_start(
                out=out[:, n + 1 - tiles : n + 1, :],
                in_=results[n // CHUNK][:, n % CHUNK + 1 - tiles : n % CHUNK + 1, :],
            )

        load_motion(0)
        load_query(0, 1)
        load_query(1, CHUNK // 2)
        load_query(2, CHUNK)
        nc.sync.dma_start(out=b_rows[:], in_=B_q.rearrange("(h o) r -> o h r", o=P))
        nc.sync.dma_start(out=a_rows[:], in_=A_q)
        load_w(0)
        load_query(3, CHUNK)
        load_w(1)
        load_motion(1)
        load_query(4, CHUNK)
        nc.vector.memset(bias_row[:], 0.0)
        nc.sync.dma_start(out=bias_row[0:1, :], in_=b_q.rearrange("(one o) -> one o", one=1))
        for c in range(LEAD, LOAD_AHEAD):
            load_query(c, CHUNK)
        for b in range(2, BATCH):
            load_motion(b)

        make_identity(nc, identity_f32[:])
        make_identity(nc, identity_bf16[:])
        nc.vector.memset(ones[:], 1.0)

        def add_chunk(c):
            for i in range(CHUNK):
                add_early(c, i)

        def turn_chunk(c):
            for i in range(CHUNK):
                turn(c, i)
                group_early(c, i)

        add_chunk(0)
        turn_chunk(0)
        add_chunk(1)
        turn_chunk(1)
        quantise(0)
        add_chunk(2)
        turn_lora()
        turn_chunk(2)
        quantise(1)
        build_w(0)
        add_chunk(3)
        turn_chunk(3)
        quantise(2)
        quantise_w(0)
        build_w(1)
        add_chunk(4)
        quantise(3)
        turn_chunk(4)
        turn_motion(1)
        quantise_w(1)
        for i in range(CHUNK):
            turn(LEAD, i)
        sort_query(LEAD + 1)
        spread_bias()

        for r in range(N_ROUNDS):
            c = r + LEAD
            tiles = range(r * ROUND, min((r + 1) * ROUND, ROWS))
            ahead = c < N_CHUNKS
            turned = tiles[1:2] if ahead and r % TURNED_EVERY == 1 else ()
            detour = [n for n in tiles if n not in turned][:DETOUR] if r < N_ROUNDS - 1 else ()
            sums = {}
            if r + LOAD_AHEAD < N_CHUNKS:
                load_query(r + LOAD_AHEAD, CHUNK)
            for n in tiles:
                if n in turned:
                    flipped = multiply_turned(n)
                else:
                    sums[n] = multiply(n, c == N_CHUNKS and n in tiles[:CHUNK])
                if n in detour:
                    nc.scalar.copy(out=result_of(n), in_=sums[n][:])
                    nc.gpsimd.tensor_tensor(
                        out=result_of(n), in0=result_of(n), in1=bias[:], op=ADD
                    )
            if c + 2 < N_CHUNKS:
                sort_query(c + 2)
            for n in turned:
                turn_back(n, flipped)
            for i in range(CHUNK):
                if c < N_CHUNKS:
                    add_motion(c, i)
                if c + 1 < N_CHUNKS:
                    turn(c + 1, i)
            if r == 0:
                quantise(LEAD - 1)
            for n in tiles:
                if n not in detour and n not in turned:
                    nc.vector.tensor_tensor(
                        out=result_of(n), in0=sums[n][:], in1=bias[:], op=ADD
                    )
                if n // CHUNK >= N_CHUNKS - LAST_CHUNKS:
                    store(n, 1)
                elif n % CHUNK == CHUNK - 1:
                    store(n, CHUNK)
            if c < N_CHUNKS:
                quantise(c)
            for b in range(2, BATCH):
                if c + 2 == b * CHUNKS_PER_BATCH:
                    turn_motion(b)
